import numpy as np
import ml_dtypes


def mxq(x, axis, fmt="e4m3"):
    dtype, down = {"e4m3": (ml_dtypes.float8_e4m3fn, 7), "e5m2": (ml_dtypes.float8_e5m2, 14)}[fmt]
    v = np.moveaxis(np.asarray(x, np.float32).astype(ml_dtypes.bfloat16).astype(np.float64), axis, -1)
    blocks = v.reshape(v.shape[:-1] + (-1, 32))
    amax = np.abs(blocks).max(-1, keepdims=True)
    byte = np.maximum(np.where(amax > 0, np.frexp(amax)[1] - 1 + 127, 0) - down, 1)
    scale = np.exp2(byte - 127.0)
    codes = (blocks / scale).astype(np.float32).astype(dtype).astype(np.float64)
    return np.moveaxis((codes * scale).reshape(v.shape), -1, axis)


WIDE = False


def mx_kscale(k):
    if not WIDE:
        return np.ones(k)
    levels = np.array([10, -10, 5, -5, 0])
    if k % 512:
        return np.exp2(np.random.permutation(np.resize(levels, k // 32))).repeat(32)
    a = np.empty((k // 512, 16))
    for p in range(k // 512):
        a[p, :8] = np.random.permutation(np.resize(levels, 8))
        for g in range(8):
            far = levels[np.abs(levels - a[p, g]) >= 10]
            a[p, g + 8] = far[np.random.randint(len(far))]
    return np.exp2(a.ravel()).repeat(32)


BF16 = ml_dtypes.bfloat16


def bf(x):
    return np.asarray(x, np.float32).astype(BF16)


def f64(x):
    return np.asarray(x).astype(np.float64)


S, HID, NH, Q_LORA, KV_LORA, NOPE, ROPE, VDIM, BLK = 8192, 512, 4, 512, 512, 64, 64, 128, 128
HEAD = NOPE + ROPE
EPS = 1e-6


def blockscale(rows, cols, k, g):
    return bf((np.random.random((rows, cols)) * 0.8 + 0.2) * g / np.sqrt(k))


def dequant(w, s):
    so = np.repeat(s, BLK, axis=0)[: w.shape[0]]
    se = np.repeat(so, BLK, axis=1)[:, : w.shape[1]]
    return w * se


def rmsnorm(x, w):
    var = np.mean(x * x, axis=-1, keepdims=True)
    return x * (1.0 / np.sqrt(var + EPS)) * w


def rotate_half(x):
    h = x.shape[-1] // 2
    return np.concatenate([-x[..., h:], x[..., :h]], axis=-1)


def setup_inputs():
    s, t = mx_kscale(HID), mx_kscale(Q_LORA)
    ang = np.arange(S)[:, None] / (10000.0 ** (np.arange(0, ROPE, 2) / ROPE))[None, :]
    ang = np.concatenate([ang, ang], axis=-1)
    return {"hidden_states": bf(np.random.standard_normal((S, HID)) * s),
            "cos": bf(np.cos(ang)),
            "sin": bf(np.sin(ang)),
            "wq_a": bf(np.random.standard_normal((Q_LORA, HID)) / s[None, :]),
            "sq_a": blockscale(Q_LORA // BLK, HID // BLK, HID, 1.0),
            "wq_b": bf(np.random.standard_normal((NH * HEAD, Q_LORA)) / t[None, :]),
            "sq_b": blockscale(NH * HEAD // BLK, Q_LORA // BLK, Q_LORA, 2.0),
            "q_ln_w": bf((1.0 + 0.1 * np.random.standard_normal(Q_LORA)) * t)}


def reference(hidden_states, cos, sin, wq_a, sq_a, wq_b, sq_b, q_ln_w):
    wa = dequant(f64(wq_a), f64(sq_a))
    lq = mxq(f64(hidden_states), 1, "e4m3") @ mxq(wa, 1, "e4m3").T
    h = rmsnorm(lq, f64(q_ln_w))
    wb = dequant(f64(wq_b), f64(sq_b))
    q = (mxq(h, 1, "e4m3") @ mxq(wb, 1, "e4m3").T).reshape(S, NH, HEAD)
    q_nope, q_pe = q[..., :NOPE], q[..., NOPE:]
    q_rot = q_pe * f64(cos)[:, None, :] + rotate_half(q_pe) * f64(sin)[:, None, :]
    return q_nope, q_rot

@@ -1,0 +1,341 @@
+from contextlib import ExitStack
+
+import concourse.mybir as mybir
+from concourse.masks import make_identity
+
+BF16 = mybir.dt.bfloat16
+F32 = mybir.dt.float32
+U32 = mybir.dt.uint32
+U8 = mybir.dt.uint8
+FP8X4 = mybir.dt.float8_e4m3fn_x4
+ACT = mybir.ActivationFunctionType
+ALU = mybir.AluOpType
+
+P = 128
+PACK = 4
+K = P * PACK
+HALVES = 2
+TOKENS = 8192
+TILES = TOKENS // P
+UNIT_TILES = 2
+UNITS = TILES // UNIT_TILES
+TABLE_UNITS = 8
+TABLE_TILES = TABLE_UNITS * UNIT_TILES
+HEADS = 4
+NOPE = 64
+ROPE = 64
+HALF = ROPE // 2
+LOW = slice(0, HALF)
+HIGH = slice(HALF, ROPE)
+OUT = HEADS * (NOPE + ROPE)
+ROW_TILES = OUT // P
+BLOCKS = K // P
+EPS = 1e-6
+WEIGHT_HALVES = ROW_TILES // UNIT_TILES
+X_LEAD = 2
+assert X_LEAD == WEIGHT_HALVES
+Q_LAG = 3
+ROTATE_LAG = Q_LAG + 1
+LQ_UNITS = 2
+PRODUCT_BUFS = 4
+WB_TRANSPOSE_ROUND = 1
+WB_QUANTISE_ROUND = 2
+
+FLOPS = 2 * 2 * TOKENS * K * OUT
+
+
+def tile_deepseekv3attention_pa_t_kernel(
+    tc, hidden_states, cos, sin, wq_a, sq_a, wq_b, sq_b, q_ln_w, out_0, out_1
+):
+    nc = tc.nc
+    x_dram = hidden_states.rearrange("(p t) k -> p t k", t=TILES)
+    cos_dram = cos.rearrange("(p t) d -> p t d", t=TILES)
+    sin_dram = sin.rearrange("(p t) d -> p t d", t=TILES)
+    nope_dram = out_0.rearrange("(p t) h d -> p t (h d)", t=TILES)
+    rot_dram = out_1.rearrange("(p t) h d -> p t (h d)", t=TILES)
+
+    with ExitStack() as ctx:
+        keep = ctx.enter_context(tc.tile_pool(name="keep", bufs=1))
+        x_pool = ctx.enter_context(tc.tile_pool(name="x", bufs=UNITS))
+        work = ctx.enter_context(tc.tile_pool(name="work", bufs=3))
+        results = ctx.enter_context(tc.tile_pool(name="results", bufs=4))
+        psum_lq = ctx.enter_context(tc.psum_pool(name="psum_lq", bufs=LQ_UNITS * UNIT_TILES))
+        psum_own = ctx.enter_context(tc.psum_pool(name="psum_own", bufs=1))
+        psum_turns = ctx.enter_context(tc.psum_pool(name="psum_turns", bufs=2))
+        ctx.enter_context(tc.manual_schedule())
+
+        sa_bc = keep.tile([P, ROW_TILES * BLOCKS], BF16)
+        nc.sync.dma_start(out=sa_bc[:], in_=sq_a.rearrange("a b -> (a b)").partition_broadcast(P))
+        wa_raw = keep.tile([P, ROW_TILES, K], BF16)
+        wa_dram = wq_a.rearrange("(o p) i -> p o i", p=P)
+        for o in range(ROW_TILES):
+            nc.sync.dma_start(out=wa_raw[:, o, :], in_=wa_dram[:, o, :])
+        x_loads = []
+        cos_loads = []
+        sin_loads = []
+
+        def load_x(n):
+            x_sb = x_pool.tile([P, UNIT_TILES, K], BF16)
+            nc.sync.dma_start(out=x_sb[:], in_=x_dram[:, n * UNIT_TILES : (n + 1) * UNIT_TILES, :])
+            x_loads.append(x_sb)
+
+        def load_tables(q):
+            tiles = slice(q * TABLE_TILES, (q + 1) * TABLE_TILES)
+            cos_sb = keep.tile([P, TABLE_TILES, ROPE], BF16, name="cos_%d" % q)
+            nc.sync.dma_start(out=cos_sb[:], in_=cos_dram[:, tiles, :])
+            cos_loads.append(cos_sb)
+            sin_sb = keep.tile([P, TABLE_TILES, ROPE], BF16, name="sin_%d" % q)
+            nc.sync.dma_start(out=sin_sb[:], in_=sin_dram[:, tiles, :])
+            sin_loads.append(sin_sb)
+
+        load_x(0)
+        sb_bc = keep.tile([P, ROW_TILES * BLOCKS], BF16)
+        nc.sync.dma_start(out=sb_bc[:], in_=sq_b.rearrange("a b -> (a b)").partition_broadcast(P))
+        wb_raw = keep.tile([P, ROW_TILES, K], BF16)
+        nc.sync.dma_start(out=wb_raw[:], in_=wq_b.rearrange("(o p) i -> p o i", p=P))
+        for n in range(1, ROTATE_LAG):
+            load_x(n)
+        gain_bc = keep.tile([P, K], BF16)
+        nc.sync.dma_start(out=gain_bc[:], in_=q_ln_w.partition_broadcast(P))
+        for n in range(ROTATE_LAG, UNITS):
+            load_x(n)
+            if n % TABLE_UNITS == ROTATE_LAG:
+                load_tables(n // TABLE_UNITS)
+
+        ident = keep.tile([P, P], F32)
+        make_identity(nc, ident[:])
+        eps = keep.tile([P, 1], F32)
+        nc.vector.memset(eps[:], EPS)
+        warm = keep.tile([P, 1], F32)
+        nc.scalar.activation(out=warm[:], in_=eps[:], func=ACT.Sqrt)
+
+        def transpose_rows(kind, rows):
+            if kind == 0:
+                bank = psum_turns.tile([P, UNIT_TILES, HALVES, P], F32, tag="turns")
+            else:
+                bank = psum_own.tile([P, UNIT_TILES, HALVES, P], F32, tag="words_h")
+            for j in range(UNIT_TILES):
+                row_words = rows[:, j, :].bitcast(F32)
+                for u in range(HALVES):
+                    nc.tensor.transpose(bank[:, j, u, :], row_words[:, u::HALVES], ident[:])
+            return bank
+
+        def scale_weight(engine, label, raw, factors):
+            scaled = keep.tile([P, ROW_TILES, K], BF16, name="scaled_" + label)
+            for o in range(ROW_TILES):
+                engine.tensor_tensor(
+                    out=scaled[:, o, :].rearrange("p (b c) -> p b c", c=P),
+                    in0=raw[:, o, :].rearrange("p (b c) -> p b c", c=P),
+                    in1=factors[:, o * BLOCKS : (o + 1) * BLOCKS].unsqueeze(2).to_broadcast([P, BLOCKS, P]),
+                    op=ALU.mult,
+                )
+            return scaled
+
+        def transpose_weight(grouped, scaled, column_order, m):
+            columns = grouped[:].bitcast(F32).rearrange(column_order, o=ROW_TILES, c=2)
+            bank = transpose_rows(m, scaled[:, m * UNIT_TILES : (m + 1) * UNIT_TILES, :])
+            for j in range(UNIT_TILES):
+                nc.scalar.copy(
+                    out=columns[:, m * UNIT_TILES + j],
+                    in_=bank[:, j].rearrange("p u (c d) -> p c d u", c=2),
+                )
+
+        def quantise_weight(grouped, codes, scales, columns):
+            nc.vector.quantize_mx(
+                out=codes[:, columns].bitcast(FP8X4),
+                scales=scales[:, columns],
+                in_=grouped[:, columns, :].rearrange("p r t -> p (r t)"),
+            )
+
+        wa_grouped = keep.tile([P, OUT, PACK], BF16, align_bytes=64)
+        wa_codes = keep.tile([P, OUT], U32, align_bytes=64)
+        wa_scales = keep.tile([P, OUT], U8, align_bytes=64)
+        wb_grouped = keep.tile([P, OUT, PACK], BF16, align_bytes=64)
+        wb_codes = keep.tile([P, OUT], U32, align_bytes=64)
+        wb_scales = keep.tile([P, OUT], U8, align_bytes=64)
+
+        words_of = {}
+        grouped_of = {}
+        codes_of = {}
+        lq_of = {}
+        sums_of = {}
+        rms_of = {}
+        inverse_of = {}
+        rot_of = {}
+        h_of = {}
+        rope_of = {}
+        plain_of = {}
+
+        def transpose_unit(kind, n, rows):
+            words_of[(kind, n)] = transpose_rows(kind, rows)
+
+        def group_unit(kind, n):
+            bank = words_of[(kind, n)]
+            grouped = work.tile([P, UNIT_TILES, P, PACK], BF16, tag="grouped_%d" % kind, align_bytes=64)
+            nc.scalar.copy(out=grouped[:].bitcast(F32), in_=bank[:].rearrange("p j u r -> p j r u"))
+            grouped_of[(kind, n)] = grouped
+
+        def quantise_unit(kind, n):
+            grouped = grouped_of[(kind, n)]
+            codes = work.tile([P, UNIT_TILES * P], U32, tag="codes_%d" % kind, align_bytes=64)
+            scales = work.tile([P, UNIT_TILES * P], U8, tag="scales_%d" % kind, align_bytes=64)
+            nc.vector.quantize_mx(
+                out=codes[:].bitcast(FP8X4),
+                scales=scales[:],
+                in_=grouped[:].rearrange("p j r t -> p (j r t)"),
+            )
+            codes_of[(kind, n)] = (codes, scales)
+
+        def multiply(out, codes, scales, j, w_codes, w_scales, columns):
+            tokens = slice(j * P, (j + 1) * P)
+            nc.tensor.matmul_mx(
+                out=out,
+                lhsT=codes[:, tokens].bitcast(FP8X4),
+                lhsT_scale=scales[:, tokens],
+                rhs=w_codes[:, columns].bitcast(FP8X4),
+                rhs_scale=w_scales[:, columns],
+                start=True,
+                stop=True,
+            )
+
+        def first_matmul(n):
+            codes, scales = codes_of[(0, n)]
+            banks = []
+            for j in range(UNIT_TILES):
+                lq = psum_lq.tile([P, OUT], F32)
+                multiply(lq[:], codes, scales, j, wa_codes, wa_scales, slice(0, OUT))
+                banks.append(lq)
+            lq_of[n] = banks
+
+        def sum_squares(n):
+            sums = work.tile([P, UNIT_TILES], F32, tag="sums")
+            for j in range(UNIT_TILES):
+                squares = work.tile([P, OUT], BF16, tag="squares")
+                nc.scalar.activation(
+                    out=squares[:], in_=lq_of[n][j][:], func=ACT.Square, accum_out=sums[:, j : j + 1]
+                )
+            sums_of[n] = sums
+
+        def root(n):
+            rms = work.tile([P, UNIT_TILES], F32, tag="rms")
+            nc.scalar.activation(out=rms[:], in_=sums_of[n][:], func=ACT.Sqrt, bias=eps[:], scale=1.0 / OUT)
+            rms_of[n] = rms
+
+        def invert(n):
+            inverse = work.tile([P, UNIT_TILES], F32, tag="inverse")
+            nc.vector.reciprocal(out=inverse[:], in_=rms_of[n][:])
+            inverse_of[n] = inverse
+
+        def normalise(n):
+            inverse = inverse_of[n]
+            h = work.tile([P, UNIT_TILES, K], BF16, tag="h")
+            banks = lq_of[n]
+            for j in range(UNIT_TILES):
+                nc.vector.scalar_tensor_tensor(
+                    out=h[:, j, :],
+                    in0=banks[j][:],
+                    scalar=inverse[:, j : j + 1],
+                    in1=gain_bc[:],
+                    op0=ALU.mult,
+                    op1=ALU.mult,
+                )
+            h_of[n] = h
+
+        def second_matmul_rotated(n):
+            codes, scales = codes_of[(1, n)]
+            rope = psum_turns.tile([P, UNIT_TILES, HEADS, ROPE], F32, tag="turns")
+            for j in range(UNIT_TILES):
+                multiply(
+                    rope[:, j].rearrange("p h d -> p (h d)"),
+                    codes, scales, j, wb_codes, wb_scales, slice(HEADS * NOPE, OUT),
+                )
+            rope_of[n] = rope
+
+        def second_matmul_plain(n):
+            codes, scales = codes_of[(1, n)]
+            plain = psum_own.tile([P, UNIT_TILES, HEADS * NOPE], F32, tag="plain")
+            for j in range(UNIT_TILES):
+                multiply(plain[:, j, :], codes, scales, j, wb_codes, wb_scales, slice(0, HEADS * NOPE))
+            plain_of[n] = plain
+
+        def store_plain(n):
+            tiles = slice(n * UNIT_TILES, (n + 1) * UNIT_TILES)
+            nope_sb = results.tile([P, UNIT_TILES, HEADS * NOPE], F32, tag="nope")
+            nc.scalar.copy(out=nope_sb[:], in_=plain_of[n][:])
+            nc.sync.dma_start(out=nope_dram[:, tiles, :], in_=nope_sb[:])
+
+        def rotate(n, here, there, sum_op):
+            first = (n * UNIT_TILES) % TABLE_TILES
+            piece = (n * UNIT_TILES) // TABLE_TILES
+            shape = [P, UNIT_TILES, HEADS, ROPE]
+            cos_bc = cos_loads[piece][:, first : first + UNIT_TILES, :].unsqueeze(2).to_broadcast(shape)
+            sin_bc = sin_loads[piece][:, first : first + UNIT_TILES, :].unsqueeze(2).to_broadcast(shape)
+            rope = rope_of[n]
+            half_shape = [P, UNIT_TILES, HEADS, HALF]
+            straight = work.tile(half_shape, F32, tag="straight", bufs=PRODUCT_BUFS)
+            nc.vector.tensor_tensor(
+                out=straight[:], in0=rope[:, :, :, here], in1=cos_bc[:, :, :, here], op=ALU.mult
+            )
+            crossed = work.tile(half_shape, F32, tag="crossed", bufs=PRODUCT_BUFS)
+            nc.vector.tensor_tensor(
+                out=crossed[:], in0=rope[:, :, :, there], in1=sin_bc[:, :, :, here], op=ALU.mult
+            )
+            nc.gpsimd.tensor_tensor(out=rot_of[n][:, :, :, here], in0=straight[:], in1=crossed[:], op=sum_op)
+
+        def rotate_low(n):
+            rot_of[n] = results.tile([P, UNIT_TILES, HEADS, ROPE], F32, name="rot_sb", tag="rot")
+            rotate(n, LOW, HIGH, ALU.subtract)
+
+        def rotate_high(n):
+            rotate(n, HIGH, LOW, ALU.add)
+            tiles = slice(n * UNIT_TILES, (n + 1) * UNIT_TILES)
+            nc.sync.dma_start(out=rot_dram[:, tiles, :], in_=rot_of[n][:].rearrange("p t h d -> p t (h d)"))
+
+        wa_scaled = scale_weight(nc.vector, "wa", wa_raw, sa_bc)
+        for m in range(WEIGHT_HALVES):
+            transpose_weight(wa_grouped, wa_scaled, "p (o c d) u -> p o c d u", m)
+            quantise_weight(wa_grouped, wa_codes, wa_scales, slice(m * UNIT_TILES * P, (m + 1) * UNIT_TILES * P))
+            transpose_unit(0, m, x_loads[m][:])
+            group_unit(0, m)
+        wb_scaled = scale_weight(nc.gpsimd, "wb", wb_raw, sb_bc)
+
+        def active(n):
+            return 0 <= n < UNITS
+
+        for i in range(UNITS + ROTATE_LAG):
+            if active(i - Q_LAG):
+                quantise_unit(1, i - Q_LAG)
+            if active(i):
+                quantise_unit(0, i)
+            if active(i - ROTATE_LAG):
+                rotate_low(i - ROTATE_LAG)
+            if active(i - 1):
+                invert(i - 1)
+            if active(i - ROTATE_LAG):
+                rotate_high(i - ROTATE_LAG)
+            if active(i - 1):
+                normalise(i - 1)
+            if active(i):
+                first_matmul(i)
+            if active(i - Q_LAG):
+                second_matmul_plain(i - Q_LAG)
+                second_matmul_rotated(i - Q_LAG)
+            if active(i + X_LEAD):
+                transpose_unit(0, i + X_LEAD, x_loads[i + X_LEAD][:])
+            if active(i - 1):
+                transpose_unit(1, i - 1, h_of[i - 1][:])
+            if active(i):
+                sum_squares(i)
+            if active(i - Q_LAG):
+                store_plain(i - Q_LAG)
+            if active(i):
+                root(i)
+            if active(i + X_LEAD):
+                group_unit(0, i + X_LEAD)
+            if active(i - 1):
+                group_unit(1, i - 1)
+            if i == WB_TRANSPOSE_ROUND:
+                for m in range(WEIGHT_HALVES):
+                    transpose_weight(wb_grouped, wb_scaled, "p (c o d) u -> p o c d u", m)
+            if i == WB_QUANTISE_ROUND:
+                quantise_weight(wb_grouped, wb_codes, wb_scales, slice(0, OUT))

@@ -89,14 +89,14 @@ def tile_deepseekv3attention_pa_t_kernel(
             sin_loads.append(sin_sb)
 
         load_x(0)
+        gain_bc = keep.tile([P, K], BF16)
+        nc.sync.dma_start(out=gain_bc[:], in_=q_ln_w.partition_broadcast(P))
         sb_bc = keep.tile([P, ROW_TILES * BLOCKS], BF16)
         nc.sync.dma_start(out=sb_bc[:], in_=sq_b.rearrange("a b -> (a b)").partition_broadcast(P))
         wb_raw = keep.tile([P, ROW_TILES, K], BF16)
         nc.sync.dma_start(out=wb_raw[:], in_=wq_b.rearrange("(o p) i -> p o i", p=P))
         for n in range(1, ROTATE_LAG):
             load_x(n)
-        gain_bc = keep.tile([P, K], BF16)
-        nc.sync.dma_start(out=gain_bc[:], in_=q_ln_w.partition_broadcast(P))
         for n in range(ROTATE_LAG, UNITS):
             load_x(n)
             if n % TABLE_UNITS == ROTATE_LAG:
@@ -107,9 +107,9 @@ def tile_deepseekv3attention_pa_t_kernel(
         eps = keep.tile([P, 1], F32)
         nc.vector.memset(eps[:], EPS)
         warm = keep.tile([P, 1], F32)
-        nc.scalar.activation(out=warm[:], in_=eps[:], func=ACT.Sqrt)
+        nc.scalar.activation(out=warm[:], in_=eps[:], func=ACT.Abs_reciprocal_sqrt)
 
-        def transpose_rows(kind, rows):
+        def transpose_rows(kind, rows, split):
             if kind == 0:
                 bank = psum_turns.tile([P, UNIT_TILES, HALVES, P], F32, tag="turns")
             else:
@@ -117,7 +117,8 @@ def tile_deepseekv3attention_pa_t_kernel(
             for j in range(UNIT_TILES):
                 row_words = rows[:, j, :].bitcast(F32)
                 for u in range(HALVES):
-                    nc.tensor.transpose(bank[:, j, u, :], row_words[:, u::HALVES], ident[:])
+                    words = row_words[:, u * P : (u + 1) * P] if split else row_words[:, u::HALVES]
+                    nc.tensor.transpose(bank[:, j, u, :], words, ident[:])
             return bank
 
         def scale_weight(engine, label, raw, factors):
@@ -131,13 +132,23 @@ def tile_deepseekv3attention_pa_t_kernel(
                 )
             return scaled
 
-        def transpose_weight(grouped, scaled, column_order, m):
-            columns = grouped[:].bitcast(F32).rearrange(column_order, o=ROW_TILES, c=2)
-            bank = transpose_rows(m, scaled[:, m * UNIT_TILES : (m + 1) * UNIT_TILES, :])
+        def transpose_wa(m):
+            columns = wa_grouped[:].bitcast(F32).rearrange(
+                "p (u o q e) w -> p o u q e w", u=HALVES, o=ROW_TILES, e=2
+            )
+            bank = transpose_rows(m, wa_scaled[:, m * UNIT_TILES : (m + 1) * UNIT_TILES, :], False)
+            for j in range(UNIT_TILES):
+                words = bank[:, j].rearrange("p w (q u e) -> p u q e w", u=HALVES, e=2)
+                for u in range(HALVES):
+                    nc.scalar.copy(out=columns[:, m * UNIT_TILES + j, u], in_=words[:, u])
+
+        def transpose_wb(m):
+            columns = wb_grouped[:].bitcast(F32).rearrange("p (c o d) w -> p o c d w", c=2, o=ROW_TILES)
+            bank = transpose_rows(m, wb_scaled[:, m * UNIT_TILES : (m + 1) * UNIT_TILES, :], False)
             for j in range(UNIT_TILES):
                 nc.scalar.copy(
                     out=columns[:, m * UNIT_TILES + j],
-                    in_=bank[:, j].rearrange("p u (c d) -> p c d u", c=2),
+                    in_=bank[:, j].rearrange("p w (c d) -> p c d w", c=2),
                 )
 
         def quantise_weight(grouped, codes, scales, columns):
@@ -154,12 +165,14 @@ def tile_deepseekv3attention_pa_t_kernel(
         wb_codes = keep.tile([P, OUT], U32, align_bytes=64)
         wb_scales = keep.tile([P, OUT], U8, align_bytes=64)
 
+        def active(n):
+            return 0 <= n < UNITS
+
         words_of = {}
         grouped_of = {}
         codes_of = {}
         lq_of = {}
         sums_of = {}
-        rms_of = {}
         inverse_of = {}
         rot_of = {}
         h_of = {}
@@ -167,31 +180,35 @@ def tile_deepseekv3attention_pa_t_kernel(
         plain_of = {}
 
         def transpose_unit(kind, n, rows):
-            words_of[(kind, n)] = transpose_rows(kind, rows)
+            words_of[(kind, n)] = transpose_rows(kind, rows, kind == 1)
 
         def group_unit(kind, n):
             bank = words_of[(kind, n)]
-            grouped = work.tile([P, UNIT_TILES, P, PACK], BF16, tag="grouped_%d" % kind, align_bytes=64)
-            nc.scalar.copy(out=grouped[:].bitcast(F32), in_=bank[:].rearrange("p j u r -> p j r u"))
-            grouped_of[(kind, n)] = grouped
-
-        def quantise_unit(kind, n):
-            grouped = grouped_of[(kind, n)]
-            codes = work.tile([P, UNIT_TILES * P], U32, tag="codes_%d" % kind, align_bytes=64)
-            scales = work.tile([P, UNIT_TILES * P], U8, tag="scales_%d" % kind, align_bytes=64)
-            nc.vector.quantize_mx(
-                out=codes[:].bitcast(FP8X4),
-                scales=scales[:],
-                in_=grouped[:].rearrange("p j r t -> p (j r t)"),
+            i = n + kind * Q_LAG
+            if i not in grouped_of:
+                grouped_of[i] = work.tile([P, 2, UNIT_TILES, P, PACK], BF16, name="grouped", align_bytes=64)
+            nc.scalar.copy(
+                out=grouped_of[i][:, kind].bitcast(F32), in_=bank[:].rearrange("p j u r -> p j r u")
             )
-            codes_of[(kind, n)] = (codes, scales)
 
-        def multiply(out, codes, scales, j, w_codes, w_scales, columns):
+        def quantise(i):
+            kinds = slice(0 if active(i) else 1, 2 if active(i - Q_LAG) else 1)
+            codes = work.tile([P, 2, UNIT_TILES * P], U32, tag="codes", align_bytes=64)
+            scales = work.tile([P, 2, UNIT_TILES * P], U8, tag="scales", align_bytes=64)
+            nc.vector.quantize_mx(
+                out=codes[:, kinds].rearrange("p k r -> p (k r)").bitcast(FP8X4),
+                scales=scales[:, kinds].rearrange("p k r -> p (k r)"),
+                in_=grouped_of[i][:, kinds].rearrange("p k j r t -> p (k j r t)"),
+            )
+            codes_of[i] = (codes, scales)
+
+        def multiply(out, kind, n, j, w_codes, w_scales, columns):
+            codes, scales = codes_of[n + kind * Q_LAG]
             tokens = slice(j * P, (j + 1) * P)
             nc.tensor.matmul_mx(
                 out=out,
-                lhsT=codes[:, tokens].bitcast(FP8X4),
-                lhsT_scale=scales[:, tokens],
+                lhsT=codes[:, kind, tokens].bitcast(FP8X4),
+                lhsT_scale=scales[:, kind, tokens],
                 rhs=w_codes[:, columns].bitcast(FP8X4),
                 rhs_scale=w_scales[:, columns],
                 start=True,
@@ -199,11 +216,10 @@ def tile_deepseekv3attention_pa_t_kernel(
             )
 
         def first_matmul(n):
-            codes, scales = codes_of[(0, n)]
             banks = []
             for j in range(UNIT_TILES):
                 lq = psum_lq.tile([P, OUT], F32)
-                multiply(lq[:], codes, scales, j, wa_codes, wa_scales, slice(0, OUT))
+                multiply(lq[:], 0, n, j, wa_codes, wa_scales, slice(0, OUT))
                 banks.append(lq)
             lq_of[n] = banks
 
@@ -216,14 +232,11 @@ def tile_deepseekv3attention_pa_t_kernel(
                 )
             sums_of[n] = sums
 
-        def root(n):
-            rms = work.tile([P, UNIT_TILES], F32, tag="rms")
-            nc.scalar.activation(out=rms[:], in_=sums_of[n][:], func=ACT.Sqrt, bias=eps[:], scale=1.0 / OUT)
-            rms_of[n] = rms
-
         def invert(n):
             inverse = work.tile([P, UNIT_TILES], F32, tag="inverse")
-            nc.vector.reciprocal(out=inverse[:], in_=rms_of[n][:])
+            nc.scalar.activation(
+                out=inverse[:], in_=sums_of[n][:], func=ACT.Abs_reciprocal_sqrt, bias=eps[:], scale=1.0 / OUT
+            )
             inverse_of[n] = inverse
 
         def normalise(n):
@@ -235,27 +248,25 @@ def tile_deepseekv3attention_pa_t_kernel(
                     out=h[:, j, :],
                     in0=banks[j][:],
                     scalar=inverse[:, j : j + 1],
-                    in1=gain_bc[:],
+                    in1=gain[:],
                     op0=ALU.mult,
                     op1=ALU.mult,
                 )
             h_of[n] = h
 
         def second_matmul_rotated(n):
-            codes, scales = codes_of[(1, n)]
             rope = psum_turns.tile([P, UNIT_TILES, HEADS, ROPE], F32, tag="turns")
             for j in range(UNIT_TILES):
                 multiply(
                     rope[:, j].rearrange("p h d -> p (h d)"),
-                    codes, scales, j, wb_codes, wb_scales, slice(HEADS * NOPE, OUT),
+                    1, n, j, wb_codes, wb_scales, slice(HEADS * NOPE, OUT),
                 )
             rope_of[n] = rope
 
         def second_matmul_plain(n):
-            codes, scales = codes_of[(1, n)]
             plain = psum_own.tile([P, UNIT_TILES, HEADS * NOPE], F32, tag="plain")
             for j in range(UNIT_TILES):
-                multiply(plain[:, j, :], codes, scales, j, wb_codes, wb_scales, slice(0, HEADS * NOPE))
+                multiply(plain[:, j, :], 1, n, j, wb_codes, wb_scales, slice(0, HEADS * NOPE))
             plain_of[n] = plain
 
         def store_plain(n):
@@ -293,24 +304,24 @@ def tile_deepseekv3attention_pa_t_kernel(
 
         wa_scaled = scale_weight(nc.vector, "wa", wa_raw, sa_bc)
         for m in range(WEIGHT_HALVES):
-            transpose_weight(wa_grouped, wa_scaled, "p (o c d) u -> p o c d u", m)
-            quantise_weight(wa_grouped, wa_codes, wa_scales, slice(m * UNIT_TILES * P, (m + 1) * UNIT_TILES * P))
+            transpose_wa(m)
+            for u in range(HALVES):
+                first_column = (u * WEIGHT_HALVES + m) * P
+                quantise_weight(wa_grouped, wa_codes, wa_scales, slice(first_column, first_column + P))
             transpose_unit(0, m, x_loads[m][:])
             group_unit(0, m)
+        gain = keep.tile([P, K], BF16)
+        nc.gpsimd.tensor_copy(
+            out=gain[:].rearrange("p (u q e) -> p u q e", u=HALVES, e=2),
+            in_=gain_bc[:].rearrange("p (q u e) -> p u q e", u=HALVES, e=2),
+        )
         wb_scaled = scale_weight(nc.gpsimd, "wb", wb_raw, sb_bc)
 
-        def active(n):
-            return 0 <= n < UNITS
-
         for i in range(UNITS + ROTATE_LAG):
-            if active(i - Q_LAG):
-                quantise_unit(1, i - Q_LAG)
-            if active(i):
-                quantise_unit(0, i)
+            if active(i) or active(i - Q_LAG):
+                quantise(i)
             if active(i - ROTATE_LAG):
                 rotate_low(i - ROTATE_LAG)
-            if active(i - 1):
-                invert(i - 1)
             if active(i - ROTATE_LAG):
                 rotate_high(i - ROTATE_LAG)
             if active(i - 1):
@@ -329,13 +340,13 @@ def tile_deepseekv3attention_pa_t_kernel(
             if active(i - Q_LAG):
                 store_plain(i - Q_LAG)
             if active(i):
-                root(i)
+                invert(i)
             if active(i + X_LEAD):
                 group_unit(0, i + X_LEAD)
             if active(i - 1):
                 group_unit(1, i - 1)
             if i == WB_TRANSPOSE_ROUND:
                 for m in range(WEIGHT_HALVES):
-                    transpose_weight(wb_grouped, wb_scaled, "p (c o d) u -> p o c d u", m)
+                    transpose_wb(m)
             if i == WB_QUANTISE_ROUND:
                 quantise_weight(wb_grouped, wb_codes, wb_scales, slice(0, OUT))

@@ -28,18 +28,16 @@ HALF = ROPE // 2
 LOW = slice(0, HALF)
 HIGH = slice(HALF, ROPE)
 OUT = HEADS * (NOPE + ROPE)
-ROW_TILES = OUT // P
+HALF_OUT = OUT // 2
+ROW_BLOCKS = OUT // P
 BLOCKS = K // P
 EPS = 1e-6
-WEIGHT_HALVES = ROW_TILES // UNIT_TILES
+WEIGHT_HALVES = PACK // UNIT_TILES
 X_LEAD = 2
-assert X_LEAD == WEIGHT_HALVES
 Q_LAG = 3
 ROTATE_LAG = Q_LAG + 1
 LQ_UNITS = 2
 PRODUCT_BUFS = 4
-WB_TRANSPOSE_ROUND = 1
-WB_QUANTISE_ROUND = 2
 
 FLOPS = 2 * 2 * TOKENS * K * OUT
 
@@ -64,12 +62,22 @@ def tile_deepseekv3attention_pa_t_kernel(
         psum_turns = ctx.enter_context(tc.psum_pool(name="psum_turns", bufs=2))
         ctx.enter_context(tc.manual_schedule())
 
-        sa_bc = keep.tile([P, ROW_TILES * BLOCKS], BF16)
-        nc.sync.dma_start(out=sa_bc[:], in_=sq_a.rearrange("a b -> (a b)").partition_broadcast(P))
-        wa_raw = keep.tile([P, ROW_TILES, K], BF16)
-        wa_dram = wq_a.rearrange("(o p) i -> p o i", p=P)
-        for o in range(ROW_TILES):
-            nc.sync.dma_start(out=wa_raw[:, o, :], in_=wa_dram[:, o, :])
+        def load_factors(label, dram):
+            factors = keep.tile([P, BLOCKS], BF16, name="factors_" + label)
+            for g in range(ROW_BLOCKS):
+                partitions = slice(g * P // ROW_BLOCKS, (g + 1) * P // ROW_BLOCKS)
+                nc.scalar.dma_start(
+                    out=factors[partitions, :], in_=dram[g, :].partition_broadcast(P // ROW_BLOCKS)
+                )
+            return factors
+
+        wa_factors = load_factors("wa", sq_a)
+        wb_factors = load_factors("wb", sq_b)
+        wa_raw = keep.tile([P, PACK, K], BF16)
+        wa_dram = wq_a.rearrange("(p t) i -> p t i", t=PACK)
+        for m in range(WEIGHT_HALVES):
+            rows = slice(m * UNIT_TILES, (m + 1) * UNIT_TILES)
+            nc.sync.dma_start(out=wa_raw[:, rows, :], in_=wa_dram[:, rows, :])
         x_loads = []
         cos_loads = []
         sin_loads = []
@@ -89,13 +97,12 @@ def tile_deepseekv3attention_pa_t_kernel(
             sin_loads.append(sin_sb)
 
         load_x(0)
+        load_x(1)
+        wb_raw = keep.tile([P, PACK, K], BF16)
+        nc.sync.dma_start(out=wb_raw[:], in_=wq_b.rearrange("(p t) i -> p t i", t=PACK))
         gain_bc = keep.tile([P, K], BF16)
         nc.sync.dma_start(out=gain_bc[:], in_=q_ln_w.partition_broadcast(P))
-        sb_bc = keep.tile([P, ROW_TILES * BLOCKS], BF16)
-        nc.sync.dma_start(out=sb_bc[:], in_=sq_b.rearrange("a b -> (a b)").partition_broadcast(P))
-        wb_raw = keep.tile([P, ROW_TILES, K], BF16)
-        nc.sync.dma_start(out=wb_raw[:], in_=wq_b.rearrange("(o p) i -> p o i", p=P))
-        for n in range(1, ROTATE_LAG):
+        for n in range(2, ROTATE_LAG):
             load_x(n)
         for n in range(ROTATE_LAG, UNITS):
             load_x(n)
@@ -121,35 +128,37 @@ def tile_deepseekv3attention_pa_t_kernel(
                     nc.tensor.transpose(bank[:, j, u, :], words, ident[:])
             return bank
 
-        def scale_weight(engine, label, raw, factors):
-            scaled = keep.tile([P, ROW_TILES, K], BF16, name="scaled_" + label)
-            for o in range(ROW_TILES):
-                engine.tensor_tensor(
-                    out=scaled[:, o, :].rearrange("p (b c) -> p b c", c=P),
-                    in0=raw[:, o, :].rearrange("p (b c) -> p b c", c=P),
-                    in1=factors[:, o * BLOCKS : (o + 1) * BLOCKS].unsqueeze(2).to_broadcast([P, BLOCKS, P]),
-                    op=ALU.mult,
+        def scale_weight(scaled, raw, factors, places):
+            for b in range(BLOCKS):
+                block = slice(b * P, (b + 1) * P)
+                nc.vector.tensor_scalar(
+                    out=scaled[:, places, block],
+                    in0=raw[:, places, block],
+                    scalar1=factors[:, b : b + 1],
+                    scalar2=None,
+                    op0=ALU.mult,
                 )
-            return scaled
 
         def transpose_wa(m):
-            columns = wa_grouped[:].bitcast(F32).rearrange(
-                "p (u o q e) w -> p o u q e w", u=HALVES, o=ROW_TILES, e=2
-            )
             bank = transpose_rows(m, wa_scaled[:, m * UNIT_TILES : (m + 1) * UNIT_TILES, :], False)
-            for j in range(UNIT_TILES):
-                words = bank[:, j].rearrange("p w (q u e) -> p u q e w", u=HALVES, e=2)
-                for u in range(HALVES):
-                    nc.scalar.copy(out=columns[:, m * UNIT_TILES + j, u], in_=words[:, u])
+            columns = wa_grouped[:, m * HALF_OUT : (m + 1) * HALF_OUT, :].bitcast(F32)
+            nc.scalar.copy(
+                out=columns.rearrange("p (q e) w -> p q (e w)", e=UNIT_TILES),
+                in_=bank[:].rearrange("p e w q -> p q (e w)"),
+            )
 
         def transpose_wb(m):
-            columns = wb_grouped[:].bitcast(F32).rearrange("p (c o d) w -> p o c d w", c=2, o=ROW_TILES)
-            bank = transpose_rows(m, wb_scaled[:, m * UNIT_TILES : (m + 1) * UNIT_TILES, :], False)
-            for j in range(UNIT_TILES):
-                nc.scalar.copy(
-                    out=columns[:, m * UNIT_TILES + j],
-                    in_=bank[:, j].rearrange("p w (c d) -> p c d w", c=2),
-                )
+            words_of[("wb", m)] = transpose_rows(m, wb_scaled[:, m * UNIT_TILES : (m + 1) * UNIT_TILES, :], False)
+
+        def group_wb(m):
+            bank = words_of[("wb", m)]
+            columns = wb_grouped[:].bitcast(F32).rearrange(
+                "p (c h q t) w -> p c h q (t w)", c=2, h=HEADS, t=PACK
+            )
+            words = bank[:].rearrange("p t w (h c q) -> p c h q (t w)", h=HEADS, c=2)
+            run = slice(m * UNIT_TILES * 2, (m + 1) * UNIT_TILES * 2)
+            for c in range(2):
+                nc.vector.tensor_copy(out=columns[:, c, :, :, run], in_=words[:, c])
 
         def quantise_weight(grouped, codes, scales, columns):
             nc.vector.quantize_mx(
@@ -158,6 +167,9 @@ def tile_deepseekv3attention_pa_t_kernel(
                 in_=grouped[:, columns, :].rearrange("p r t -> p (r t)"),
             )
 
+        wa_scaled = keep.tile([P, PACK, K], BF16)
+        wb_scaled = keep.tile([P, PACK, K], BF16)
+        gain = keep.tile([P, K], BF16)
         wa_grouped = keep.tile([P, OUT, PACK], BF16, align_bytes=64)
         wa_codes = keep.tile([P, OUT], U32, align_bytes=64)
         wa_scales = keep.tile([P, OUT], U8, align_bytes=64)
@@ -302,30 +314,35 @@ def tile_deepseekv3attention_pa_t_kernel(
             tiles = slice(n * UNIT_TILES, (n + 1) * UNIT_TILES)
             nc.sync.dma_start(out=rot_dram[:, tiles, :], in_=rot_of[n][:].rearrange("p t h d -> p t (h d)"))
 
-        wa_scaled = scale_weight(nc.vector, "wa", wa_raw, sa_bc)
+        for m in range(WEIGHT_HALVES):
+            scale_weight(wa_scaled, wa_raw, wa_factors, slice(m * UNIT_TILES, (m + 1) * UNIT_TILES))
         for m in range(WEIGHT_HALVES):
             transpose_wa(m)
-            for u in range(HALVES):
-                first_column = (u * WEIGHT_HALVES + m) * P
-                quantise_weight(wa_grouped, wa_codes, wa_scales, slice(first_column, first_column + P))
-            transpose_unit(0, m, x_loads[m][:])
-            group_unit(0, m)
-        gain = keep.tile([P, K], BF16)
-        nc.gpsimd.tensor_copy(
-            out=gain[:].rearrange("p (u q e) -> p u q e", u=HALVES, e=2),
-            in_=gain_bc[:].rearrange("p (q u e) -> p u q e", u=HALVES, e=2),
-        )
-        wb_scaled = scale_weight(nc.gpsimd, "wb", wb_raw, sb_bc)
+            quantise_weight(wa_grouped, wa_codes, wa_scales, slice(m * HALF_OUT, (m + 1) * HALF_OUT))
+        for n in range(X_LEAD):
+            transpose_unit(0, n, x_loads[n][:])
+            group_unit(0, n)
 
         for i in range(UNITS + ROTATE_LAG):
             if active(i) or active(i - Q_LAG):
                 quantise(i)
+            if i == 0:
+                scale_weight(wb_scaled, wb_raw, wb_factors, slice(0, PACK))
+                nc.vector.tensor_copy(
+                    out=gain[:].rearrange("p (u q e) -> p u q e", u=HALVES, e=2),
+                    in_=gain_bc[:].rearrange("p (q u e) -> p u q e", u=HALVES, e=2),
+                )
+            if i == 1:
+                for m in range(WEIGHT_HALVES):
+                    group_wb(m)
             if active(i - ROTATE_LAG):
                 rotate_low(i - ROTATE_LAG)
             if active(i - ROTATE_LAG):
                 rotate_high(i - ROTATE_LAG)
             if active(i - 1):
                 normalise(i - 1)
+            if i == 1:
+                quantise_weight(wb_grouped, wb_codes, wb_scales, slice(0, OUT))
             if active(i):
                 first_matmul(i)
             if active(i - Q_LAG):
@@ -333,6 +350,9 @@ def tile_deepseekv3attention_pa_t_kernel(
                 second_matmul_rotated(i - Q_LAG)
             if active(i + X_LEAD):
                 transpose_unit(0, i + X_LEAD, x_loads[i + X_LEAD][:])
+            if i == 0:
+                for m in range(WEIGHT_HALVES):
+                    transpose_wb(m)
             if active(i - 1):
                 transpose_unit(1, i - 1, h_of[i - 1][:])
             if active(i):
@@ -345,8 +365,3 @@ def tile_deepseekv3attention_pa_t_kernel(
                 group_unit(0, i + X_LEAD)
             if active(i - 1):
                 group_unit(1, i - 1)
-            if i == WB_TRANSPOSE_ROUND:
-                for m in range(WEIGHT_HALVES):
-                    transpose_wb(m)
-            if i == WB_QUANTISE_ROUND:
-                quantise_weight(wb_grouped, wb_codes, wb_scales, slice(0, OUT))

@@ -31,11 +31,13 @@ OUT = HEADS * (NOPE + ROPE)
 HALF_OUT = OUT // 2
 ROW_BLOCKS = OUT // P
 BLOCKS = K // P
+QUARTER = P // ROW_BLOCKS
 EPS = 1e-6
 WEIGHT_HALVES = PACK // UNIT_TILES
 X_LEAD = 2
 Q_LAG = 3
 ROTATE_LAG = Q_LAG + 1
+OWN_BANKS = {1: "words_h", 2: "plain"}
 LQ_UNITS = 2
 PRODUCT_BUFS = 4
 
@@ -63,21 +65,16 @@ def tile_deepseekv3attention_pa_t_kernel(
         ctx.enter_context(tc.manual_schedule())
 
         def load_factors(label, dram):
-            factors = keep.tile([P, BLOCKS], BF16, name="factors_" + label)
-            for g in range(ROW_BLOCKS):
-                partitions = slice(g * P // ROW_BLOCKS, (g + 1) * P // ROW_BLOCKS)
-                nc.scalar.dma_start(
-                    out=factors[partitions, :], in_=dram[g, :].partition_broadcast(P // ROW_BLOCKS)
-                )
+            factors = keep.tile([P, ROW_BLOCKS * BLOCKS], BF16, name="all_factors_" + label)
+            nc.sync.dma_start(out=factors[:], in_=dram.rearrange("a b -> (a b)").partition_broadcast(P))
             return factors
 
-        wa_factors = load_factors("wa", sq_a)
-        wb_factors = load_factors("wb", sq_b)
+        wa_all_factors = load_factors("wa", sq_a)
         wa_raw = keep.tile([P, PACK, K], BF16)
         wa_dram = wq_a.rearrange("(p t) i -> p t i", t=PACK)
         for m in range(WEIGHT_HALVES):
-            rows = slice(m * UNIT_TILES, (m + 1) * UNIT_TILES)
-            nc.sync.dma_start(out=wa_raw[:, rows, :], in_=wa_dram[:, rows, :])
+            places = slice(m * UNIT_TILES, (m + 1) * UNIT_TILES)
+            nc.sync.dma_start(out=wa_raw[:, places, :], in_=wa_dram[:, places, :])
         x_loads = []
         cos_loads = []
         sin_loads = []
@@ -97,11 +94,15 @@ def tile_deepseekv3attention_pa_t_kernel(
             sin_loads.append(sin_sb)
 
         load_x(0)
+        gain_row = keep.tile([P, K], BF16)
+        nc.vector.memset(gain_row[:], 0.0)
+        ones = keep.tile([P, P], BF16)
+        nc.vector.memset(ones[:], 1.0)
+        nc.sync.dma_start(out=gain_row[0:1, :], in_=q_ln_w.unsqueeze(0))
         load_x(1)
+        wb_all_factors = load_factors("wb", sq_b)
         wb_raw = keep.tile([P, PACK, K], BF16)
         nc.sync.dma_start(out=wb_raw[:], in_=wq_b.rearrange("(p t) i -> p t i", t=PACK))
-        gain_bc = keep.tile([P, K], BF16)
-        nc.sync.dma_start(out=gain_bc[:], in_=q_ln_w.partition_broadcast(P))
         for n in range(2, ROTATE_LAG):
             load_x(n)
         for n in range(ROTATE_LAG, UNITS):
@@ -120,13 +121,22 @@ def tile_deepseekv3attention_pa_t_kernel(
             if kind == 0:
                 bank = psum_turns.tile([P, UNIT_TILES, HALVES, P], F32, tag="turns")
             else:
-                bank = psum_own.tile([P, UNIT_TILES, HALVES, P], F32, tag="words_h")
+                bank = psum_own.tile([P, UNIT_TILES, HALVES, P], F32, name="words_bank", tag=OWN_BANKS[kind])
             for j in range(UNIT_TILES):
                 row_words = rows[:, j, :].bitcast(F32)
                 for u in range(HALVES):
                     words = row_words[:, u * P : (u + 1) * P] if split else row_words[:, u::HALVES]
                     nc.tensor.transpose(bank[:, j, u, :], words, ident[:])
             return bank
+
+        def own_factors(label, all_factors):
+            factors = keep.tile([P, BLOCKS], BF16, name="factors_" + label)
+            for g in range(ROW_BLOCKS):
+                quarter = slice(g * QUARTER, (g + 1) * QUARTER)
+                nc.vector.tensor_copy(
+                    out=factors[quarter, :], in_=all_factors[quarter, g * BLOCKS : (g + 1) * BLOCKS]
+                )
+            return factors
 
         def scale_weight(scaled, raw, factors, places):
             for b in range(BLOCKS):
@@ -142,13 +152,14 @@ def tile_deepseekv3attention_pa_t_kernel(
         def transpose_wa(m):
             bank = transpose_rows(m, wa_scaled[:, m * UNIT_TILES : (m + 1) * UNIT_TILES, :], False)
             columns = wa_grouped[:, m * HALF_OUT : (m + 1) * HALF_OUT, :].bitcast(F32)
-            nc.scalar.copy(
+            copy = nc.vector.tensor_copy if m == 0 else nc.scalar.copy
+            copy(
                 out=columns.rearrange("p (q e) w -> p q (e w)", e=UNIT_TILES),
                 in_=bank[:].rearrange("p e w q -> p q (e w)"),
             )
 
         def transpose_wb(m):
-            words_of[("wb", m)] = transpose_rows(m, wb_scaled[:, m * UNIT_TILES : (m + 1) * UNIT_TILES, :], False)
+            words_of[("wb", m)] = transpose_rows(2, wb_scaled[:, m * UNIT_TILES : (m + 1) * UNIT_TILES, :], False)
 
         def group_wb(m):
             bank = words_of[("wb", m)]
@@ -314,34 +325,37 @@ def tile_deepseekv3attention_pa_t_kernel(
             tiles = slice(n * UNIT_TILES, (n + 1) * UNIT_TILES)
             nc.sync.dma_start(out=rot_dram[:, tiles, :], in_=rot_of[n][:].rearrange("p t h d -> p t (h d)"))
 
+        wa_factors = own_factors("wa", wa_all_factors)
         for m in range(WEIGHT_HALVES):
             scale_weight(wa_scaled, wa_raw, wa_factors, slice(m * UNIT_TILES, (m + 1) * UNIT_TILES))
         for m in range(WEIGHT_HALVES):
             transpose_wa(m)
+        for m in range(WEIGHT_HALVES):
             quantise_weight(wa_grouped, wa_codes, wa_scales, slice(m * HALF_OUT, (m + 1) * HALF_OUT))
         for n in range(X_LEAD):
             transpose_unit(0, n, x_loads[n][:])
             group_unit(0, n)
+        gain_bank = psum_own.tile([P, K], F32, tag="plain")
+        nc.tensor.matmul(gain_bank[:], lhsT=ones[:], rhs=gain_row[:], start=True, stop=True)
 
         for i in range(UNITS + ROTATE_LAG):
             if active(i) or active(i - Q_LAG):
                 quantise(i)
             if i == 0:
-                scale_weight(wb_scaled, wb_raw, wb_factors, slice(0, PACK))
                 nc.vector.tensor_copy(
                     out=gain[:].rearrange("p (u q e) -> p u q e", u=HALVES, e=2),
-                    in_=gain_bc[:].rearrange("p (q u e) -> p u q e", u=HALVES, e=2),
+                    in_=gain_bank[:].rearrange("p (q u e) -> p u q e", u=HALVES, e=2),
                 )
-            if i == 1:
-                for m in range(WEIGHT_HALVES):
-                    group_wb(m)
+                scale_weight(wb_scaled, wb_raw, own_factors("wb", wb_all_factors), slice(0, PACK))
             if active(i - ROTATE_LAG):
                 rotate_low(i - ROTATE_LAG)
             if active(i - ROTATE_LAG):
                 rotate_high(i - ROTATE_LAG)
             if active(i - 1):
                 normalise(i - 1)
-            if i == 1:
+            if 1 <= i <= WEIGHT_HALVES:
+                group_wb(i - 1)
+            if i == WEIGHT_HALVES:
                 quantise_weight(wb_grouped, wb_codes, wb_scales, slice(0, OUT))
             if active(i):
                 first_matmul(i)
@@ -350,11 +364,10 @@ def tile_deepseekv3attention_pa_t_kernel(
                 second_matmul_rotated(i - Q_LAG)
             if active(i + X_LEAD):
                 transpose_unit(0, i + X_LEAD, x_loads[i + X_LEAD][:])
-            if i == 0:
-                for m in range(WEIGHT_HALVES):
-                    transpose_wb(m)
             if active(i - 1):
                 transpose_unit(1, i - 1, h_of[i - 1][:])
+            if i < WEIGHT_HALVES:
+                transpose_wb(i)
             if active(i):
                 sum_squares(i)
             if active(i - Q_LAG):

@@ -38,6 +38,7 @@ X_LEAD = 2
 Q_LAG = 3
 ROTATE_LAG = Q_LAG + 1
 OWN_BANKS = {1: "words_h", 2: "plain"}
+WARM_MATMULS = 5
 LQ_UNITS = 2
 PRODUCT_BUFS = 4
 
@@ -63,6 +64,12 @@ def tile_deepseekv3attention_pa_t_kernel(
         psum_own = ctx.enter_context(tc.psum_pool(name="psum_own", bufs=1))
         psum_turns = ctx.enter_context(tc.psum_pool(name="psum_turns", bufs=2))
         ctx.enter_context(tc.manual_schedule())
+
+        ones = keep.tile([P, K], BF16)
+        nc.vector.memset(ones[:], 1.0)
+        warm_bank = psum_own.tile([P, K], F32, tag="plain")
+        for w in range(WARM_MATMULS):
+            nc.tensor.matmul(warm_bank[:], lhsT=ones[:, :P], rhs=ones[:], start=True, stop=True)
 
         def load_factors(label, dram):
             factors = keep.tile([P, ROW_BLOCKS * BLOCKS], BF16, name="all_factors_" + label)
@@ -95,9 +102,7 @@ def tile_deepseekv3attention_pa_t_kernel(
 
         load_x(0)
         gain_row = keep.tile([P, K], BF16)
-        nc.vector.memset(gain_row[:], 0.0)
-        ones = keep.tile([P, P], BF16)
-        nc.vector.memset(ones[:], 1.0)
+        nc.gpsimd.memset(gain_row[:], 0.0)
         nc.sync.dma_start(out=gain_row[0:1, :], in_=q_ln_w.unsqueeze(0))
         load_x(1)
         wb_all_factors = load_factors("wb", sq_b)
@@ -168,8 +173,9 @@ def tile_deepseekv3attention_pa_t_kernel(
             )
             words = bank[:].rearrange("p t w (h c q) -> p c h q (t w)", h=HEADS, c=2)
             run = slice(m * UNIT_TILES * 2, (m + 1) * UNIT_TILES * 2)
+            copy = nc.vector.tensor_copy if m == 0 else nc.scalar.copy
             for c in range(2):
-                nc.vector.tensor_copy(out=columns[:, c, :, :, run], in_=words[:, c])
+                copy(out=columns[:, c, :, :, run], in_=words[:, c])
 
         def quantise_weight(grouped, codes, scales, columns):
             nc.vector.quantize_mx(
@@ -294,7 +300,7 @@ def tile_deepseekv3attention_pa_t_kernel(
 
         def store_plain(n):
             tiles = slice(n * UNIT_TILES, (n + 1) * UNIT_TILES)
-            nope_sb = results.tile([P, UNIT_TILES, HEADS * NOPE], F32, tag="nope")
+            nope_sb = results.tile([P, UNIT_TILES, HEADS * NOPE], F32, tag="nope", bufs=UNITS)
             nc.scalar.copy(out=nope_sb[:], in_=plain_of[n][:])
             nc.sync.dma_start(out=nope_dram[:, tiles, :], in_=nope_sb[:])
 
@@ -306,7 +312,7 @@ def tile_deepseekv3attention_pa_t_kernel(
             sin_bc = sin_loads[piece][:, first : first + UNIT_TILES, :].unsqueeze(2).to_broadcast(shape)
             rope = rope_of[n]
             half_shape = [P, UNIT_TILES, HEADS, HALF]
-            straight = work.tile(half_shape, F32, tag="straight", bufs=PRODUCT_BUFS)
+            straight = work.tile(half_shape, F32, tag="straight", bufs=PRODUCT_BUFS + 2)
             nc.vector.tensor_tensor(
                 out=straight[:], in0=rope[:, :, :, here], in1=cos_bc[:, :, :, here], op=ALU.mult
             )
@@ -314,7 +320,8 @@ def tile_deepseekv3attention_pa_t_kernel(
             nc.vector.tensor_tensor(
                 out=crossed[:], in0=rope[:, :, :, there], in1=sin_bc[:, :, :, here], op=ALU.mult
             )
-            nc.gpsimd.tensor_tensor(out=rot_of[n][:, :, :, here], in0=straight[:], in1=crossed[:], op=sum_op)
+            sum_engine = nc.vector if n == UNITS - 1 and here == HIGH else nc.gpsimd
+            sum_engine.tensor_tensor(out=rot_of[n][:, :, :, here], in0=straight[:], in1=crossed[:], op=sum_op)
 
         def rotate_low(n):
             rot_of[n] = results.tile([P, UNIT_TILES, HEADS, ROPE], F32, name="rot_sb", tag="rot")
@@ -336,16 +343,19 @@ def tile_deepseekv3attention_pa_t_kernel(
             transpose_unit(0, n, x_loads[n][:])
             group_unit(0, n)
         gain_bank = psum_own.tile([P, K], F32, tag="plain")
-        nc.tensor.matmul(gain_bank[:], lhsT=ones[:], rhs=gain_row[:], start=True, stop=True)
+        nc.tensor.matmul(gain_bank[:], lhsT=ones[:, :P], rhs=gain_row[:], start=True, stop=True)
+
+        nc.scalar.copy(
+            out=gain[:].rearrange("p (u q e) -> p u q e", u=HALVES, e=2),
+            in_=gain_bank[:].rearrange("p (q u e) -> p u q e", u=HALVES, e=2),
+        )
 
         for i in range(UNITS + ROTATE_LAG):
             if active(i) or active(i - Q_LAG):
                 quantise(i)
+            if i == Q_LAG:
+                quantise_weight(wb_grouped, wb_codes, wb_scales, slice(0, OUT))
             if i == 0:
-                nc.vector.tensor_copy(
-                    out=gain[:].rearrange("p (u q e) -> p u q e", u=HALVES, e=2),
-                    in_=gain_bank[:].rearrange("p (q u e) -> p u q e", u=HALVES, e=2),
-                )
                 scale_weight(wb_scaled, wb_raw, own_factors("wb", wb_all_factors), slice(0, PACK))
             if active(i - ROTATE_LAG):
                 rotate_low(i - ROTATE_LAG)
@@ -353,10 +363,8 @@ def tile_deepseekv3attention_pa_t_kernel(
                 rotate_high(i - ROTATE_LAG)
             if active(i - 1):
                 normalise(i - 1)
-            if 1 <= i <= WEIGHT_HALVES:
-                group_wb(i - 1)
-            if i == WEIGHT_HALVES:
-                quantise_weight(wb_grouped, wb_codes, wb_scales, slice(0, OUT))
+            if i == 1:
+                group_wb(0)
             if active(i):
                 first_matmul(i)
             if active(i - Q_LAG):
@@ -368,6 +376,8 @@ def tile_deepseekv3attention_pa_t_kernel(
                 transpose_unit(1, i - 1, h_of[i - 1][:])
             if i < WEIGHT_HALVES:
                 transpose_wb(i)
+            if i == 2:
+                group_wb(1)
             if active(i):
                 sum_squares(i)
             if active(i - Q_LAG):

@@ -34,12 +34,14 @@ BLOCKS = K // P
 QUARTER = P // ROW_BLOCKS
 EPS = 1e-6
 WEIGHT_HALVES = PACK // UNIT_TILES
+LOAD_LEAD = 8
 X_LEAD = 2
 Q_LAG = 3
 ROTATE_LAG = Q_LAG + 1
 OWN_BANKS = {1: "words_h", 2: "plain"}
 WARM_MATMULS = 5
 LQ_UNITS = 2
+ROT_BUFS = 8
 PRODUCT_BUFS = 4
 
 FLOPS = 2 * 2 * TOKENS * K * OUT
@@ -108,12 +110,14 @@ def tile_deepseekv3attention_pa_t_kernel(
         wb_all_factors = load_factors("wb", sq_b)
         wb_raw = keep.tile([P, PACK, K], BF16)
         nc.sync.dma_start(out=wb_raw[:], in_=wq_b.rearrange("(p t) i -> p t i", t=PACK))
-        for n in range(2, ROTATE_LAG):
-            load_x(n)
-        for n in range(ROTATE_LAG, UNITS):
+
+        def load_ahead(n):
             load_x(n)
             if n % TABLE_UNITS == ROTATE_LAG:
                 load_tables(n // TABLE_UNITS)
+
+        for n in range(2, LOAD_LEAD):
+            load_ahead(n)
 
         ident = keep.tile([P, P], F32)
         make_identity(nc, ident[:])
@@ -134,11 +138,11 @@ def tile_deepseekv3attention_pa_t_kernel(
                     nc.tensor.transpose(bank[:, j, u, :], words, ident[:])
             return bank
 
-        def own_factors(label, all_factors):
+        def own_factors(engine, label, all_factors):
             factors = keep.tile([P, BLOCKS], BF16, name="factors_" + label)
             for g in range(ROW_BLOCKS):
                 quarter = slice(g * QUARTER, (g + 1) * QUARTER)
-                nc.vector.tensor_copy(
+                engine.tensor_copy(
                     out=factors[quarter, :], in_=all_factors[quarter, g * BLOCKS : (g + 1) * BLOCKS]
                 )
             return factors
@@ -302,7 +306,8 @@ def tile_deepseekv3attention_pa_t_kernel(
             tiles = slice(n * UNIT_TILES, (n + 1) * UNIT_TILES)
             nope_sb = results.tile([P, UNIT_TILES, HEADS * NOPE], F32, tag="nope", bufs=UNITS)
             nc.scalar.copy(out=nope_sb[:], in_=plain_of[n][:])
-            nc.sync.dma_start(out=nope_dram[:, tiles, :], in_=nope_sb[:])
+            queue = nc.scalar if n == UNITS - 1 else nc.sync
+            queue.dma_start(out=nope_dram[:, tiles, :], in_=nope_sb[:])
 
         def rotate(n, here, there, sum_op):
             first = (n * UNIT_TILES) % TABLE_TILES
@@ -320,19 +325,27 @@ def tile_deepseekv3attention_pa_t_kernel(
             nc.vector.tensor_tensor(
                 out=crossed[:], in0=rope[:, :, :, there], in1=sin_bc[:, :, :, here], op=ALU.mult
             )
-            sum_engine = nc.vector if n == UNITS - 1 and here == HIGH else nc.gpsimd
-            sum_engine.tensor_tensor(out=rot_of[n][:, :, :, here], in0=straight[:], in1=crossed[:], op=sum_op)
 
-        def rotate_low(n):
-            rot_of[n] = results.tile([P, UNIT_TILES, HEADS, ROPE], F32, name="rot_sb", tag="rot")
-            rotate(n, LOW, HIGH, ALU.subtract)
+            def add_up(engine):
+                engine.tensor_tensor(out=rot_of[n][:, :, :, here], in0=straight[:], in1=crossed[:], op=sum_op)
 
-        def rotate_high(n):
-            rotate(n, HIGH, LOW, ALU.add)
+            return add_up
+
+        def rotate_unit(n):
+            rot_of[n] = results.tile([P, UNIT_TILES, HEADS, ROPE], F32, name="rot_sb", tag="rot", bufs=ROT_BUFS)
+            add_low = rotate(n, LOW, HIGH, ALU.subtract)
+            if n < UNITS - 1:
+                add_low(nc.gpsimd)
+            add_high = rotate(n, HIGH, LOW, ALU.add)
+            if n < UNITS - 1:
+                add_high(nc.gpsimd)
+            else:
+                add_low(nc.vector)
+                add_high(nc.vector)
             tiles = slice(n * UNIT_TILES, (n + 1) * UNIT_TILES)
             nc.sync.dma_start(out=rot_dram[:, tiles, :], in_=rot_of[n][:].rearrange("p t h d -> p t (h d)"))
 
-        wa_factors = own_factors("wa", wa_all_factors)
+        wa_factors = own_factors(nc.vector, "wa", wa_all_factors)
         for m in range(WEIGHT_HALVES):
             scale_weight(wa_scaled, wa_raw, wa_factors, slice(m * UNIT_TILES, (m + 1) * UNIT_TILES))
         for m in range(WEIGHT_HALVES):
@@ -351,20 +364,20 @@ def tile_deepseekv3attention_pa_t_kernel(
         )
 
         for i in range(UNITS + ROTATE_LAG):
+            if active(i + LOAD_LEAD):
+                load_ahead(i + LOAD_LEAD)
             if active(i) or active(i - Q_LAG):
                 quantise(i)
             if i == Q_LAG:
                 quantise_weight(wb_grouped, wb_codes, wb_scales, slice(0, OUT))
             if i == 0:
-                scale_weight(wb_scaled, wb_raw, own_factors("wb", wb_all_factors), slice(0, PACK))
+                scale_weight(wb_scaled, wb_raw, own_factors(nc.gpsimd, "wb", wb_all_factors), slice(0, PACK))
             if active(i - ROTATE_LAG):
-                rotate_low(i - ROTATE_LAG)
-            if active(i - ROTATE_LAG):
-                rotate_high(i - ROTATE_LAG)
-            if active(i - 1):
-                normalise(i - 1)
+                rotate_unit(i - ROTATE_LAG)
             if i == 1:
                 group_wb(0)
+            if active(i - 1):
+                normalise(i - 1)
             if active(i):
                 first_matmul(i)
             if active(i - Q_LAG):

from contextlib import ExitStack

import concourse.mybir as mybir
from concourse.masks import make_identity

BF16 = mybir.dt.bfloat16
F32 = mybir.dt.float32
U32 = mybir.dt.uint32
U8 = mybir.dt.uint8
FP8X4 = mybir.dt.float8_e4m3fn_x4
ACT = mybir.ActivationFunctionType
ALU = mybir.AluOpType

P = 128
PACK = 4
K = P * PACK
HALVES = 2
TOKENS = 8192
TILES = TOKENS // P
UNIT_TILES = 2
UNITS = TILES // UNIT_TILES
TABLE_UNITS = 8
TABLE_TILES = TABLE_UNITS * UNIT_TILES
HEADS = 4
NOPE = 64
ROPE = 64
HALF = ROPE // 2
LOW = slice(0, HALF)
HIGH = slice(HALF, ROPE)
OUT = HEADS * (NOPE + ROPE)
HALF_OUT = OUT // 2
ROW_BLOCKS = OUT // P
BLOCKS = K // P
QUARTER = P // ROW_BLOCKS
EPS = 1e-6
WEIGHT_HALVES = PACK // UNIT_TILES
LOAD_LEAD = 8
X_LEAD = 2
Q_LAG = 3
ROTATE_LAG = Q_LAG + 1
OWN_BANKS = {1: "words_h", 2: "plain"}
WARM_MATMULS = 5
LQ_UNITS = 2
ROT_BUFS = 8
PRODUCT_BUFS = 4

FLOPS = 2 * 2 * TOKENS * K * OUT


def tile_deepseekv3attention_pa_t_kernel(
    tc, hidden_states, cos, sin, wq_a, sq_a, wq_b, sq_b, q_ln_w, out_0, out_1
):
    nc = tc.nc
    x_dram = hidden_states.rearrange("(p t) k -> p t k", t=TILES)
    cos_dram = cos.rearrange("(p t) d -> p t d", t=TILES)
    sin_dram = sin.rearrange("(p t) d -> p t d", t=TILES)
    nope_dram = out_0.rearrange("(p t) h d -> p t (h d)", t=TILES)
    rot_dram = out_1.rearrange("(p t) h d -> p t (h d)", t=TILES)

    with ExitStack() as ctx:
        keep = ctx.enter_context(tc.tile_pool(name="keep", bufs=1))
        x_pool = ctx.enter_context(tc.tile_pool(name="x", bufs=UNITS))
        work = ctx.enter_context(tc.tile_pool(name="work", bufs=3))
        results = ctx.enter_context(tc.tile_pool(name="results", bufs=4))
        psum_lq = ctx.enter_context(tc.psum_pool(name="psum_lq", bufs=LQ_UNITS * UNIT_TILES))
        psum_own = ctx.enter_context(tc.psum_pool(name="psum_own", bufs=1))
        psum_turns = ctx.enter_context(tc.psum_pool(name="psum_turns", bufs=2))
        ctx.enter_context(tc.manual_schedule())

        ones = keep.tile([P, K], BF16)
        nc.vector.memset(ones[:], 1.0)
        warm_bank = psum_own.tile([P, K], F32, tag="plain")
        for w in range(WARM_MATMULS):
            nc.tensor.matmul(warm_bank[:], lhsT=ones[:, :P], rhs=ones[:], start=True, stop=True)

        def load_factors(label, dram):
            factors = keep.tile([P, ROW_BLOCKS * BLOCKS], BF16, name="all_factors_" + label)
            nc.sync.dma_start(out=factors[:], in_=dram.rearrange("a b -> (a b)").partition_broadcast(P))
            return factors

        wa_all_factors = load_factors("wa", sq_a)
        wa_raw = keep.tile([P, PACK, K], BF16)
        wa_dram = wq_a.rearrange("(p t) i -> p t i", t=PACK)
        for m in range(WEIGHT_HALVES):
            places = slice(m * UNIT_TILES, (m + 1) * UNIT_TILES)
            nc.sync.dma_start(out=wa_raw[:, places, :], in_=wa_dram[:, places, :])
        x_loads = []
        cos_loads = []
        sin_loads = []

        def load_x(n):
            x_sb = x_pool.tile([P, UNIT_TILES, K], BF16)
            nc.sync.dma_start(out=x_sb[:], in_=x_dram[:, n * UNIT_TILES : (n + 1) * UNIT_TILES, :])
            x_loads.append(x_sb)

        def load_tables(q):
            tiles = slice(q * TABLE_TILES, (q + 1) * TABLE_TILES)
            cos_sb = keep.tile([P, TABLE_TILES, ROPE], BF16, name="cos_%d" % q)
            nc.sync.dma_start(out=cos_sb[:], in_=cos_dram[:, tiles, :])
            cos_loads.append(cos_sb)
            sin_sb = keep.tile([P, TABLE_TILES, ROPE], BF16, name="sin_%d" % q)
            nc.sync.dma_start(out=sin_sb[:], in_=sin_dram[:, tiles, :])
            sin_loads.append(sin_sb)

        load_x(0)
        gain_row = keep.tile([P, K], BF16)
        nc.gpsimd.memset(gain_row[:], 0.0)
        nc.sync.dma_start(out=gain_row[0:1, :], in_=q_ln_w.unsqueeze(0))
        load_x(1)
        wb_all_factors = load_factors("wb", sq_b)
        wb_raw = keep.tile([P, PACK, K], BF16)
        nc.sync.dma_start(out=wb_raw[:], in_=wq_b.rearrange("(p t) i -> p t i", t=PACK))

        def load_ahead(n):
            load_x(n)
            if n % TABLE_UNITS == ROTATE_LAG:
                load_tables(n // TABLE_UNITS)

        for n in range(2, LOAD_LEAD):
            load_ahead(n)

        ident = keep.tile([P, P], F32)
        make_identity(nc, ident[:])
        eps = keep.tile([P, 1], F32)
        nc.vector.memset(eps[:], EPS)
        warm = keep.tile([P, 1], F32)
        nc.scalar.activation(out=warm[:], in_=eps[:], func=ACT.Abs_reciprocal_sqrt)

        def transpose_rows(kind, rows, split):
            if kind == 0:
                bank = psum_turns.tile([P, UNIT_TILES, HALVES, P], F32, tag="turns")
            else:
                bank = psum_own.tile([P, UNIT_TILES, HALVES, P], F32, name="words_bank", tag=OWN_BANKS[kind])
            for j in range(UNIT_TILES):
                row_words = rows[:, j, :].bitcast(F32)
                for u in range(HALVES):
                    words = row_words[:, u * P : (u + 1) * P] if split else row_words[:, u::HALVES]
                    nc.tensor.transpose(bank[:, j, u, :], words, ident[:])
            return bank

        def own_factors(engine, label, all_factors):
            factors = keep.tile([P, BLOCKS], BF16, name="factors_" + label)
            for g in range(ROW_BLOCKS):
                quarter = slice(g * QUARTER, (g + 1) * QUARTER)
                engine.tensor_copy(
                    out=factors[quarter, :], in_=all_factors[quarter, g * BLOCKS : (g + 1) * BLOCKS]
                )
            return factors

        def scale_weight(scaled, raw, factors, places):
            for b in range(BLOCKS):
                block = slice(b * P, (b + 1) * P)
                nc.vector.tensor_scalar(
                    out=scaled[:, places, block],
                    in0=raw[:, places, block],
                    scalar1=factors[:, b : b + 1],
                    scalar2=None,
                    op0=ALU.mult,
                )

        def transpose_wa(m):
            bank = transpose_rows(m, wa_scaled[:, m * UNIT_TILES : (m + 1) * UNIT_TILES, :], False)
            columns = wa_grouped[:, m * HALF_OUT : (m + 1) * HALF_OUT, :].bitcast(F32)
            copy = nc.vector.tensor_copy if m == 0 else nc.scalar.copy
            copy(
                out=columns.rearrange("p (q e) w -> p q (e w)", e=UNIT_TILES),
                in_=bank[:].rearrange("p e w q -> p q (e w)"),
            )

        def transpose_wb(m):
            words_of[("wb", m)] = transpose_rows(2, wb_scaled[:, m * UNIT_TILES : (m + 1) * UNIT_TILES, :], False)

        def group_wb(m):
            bank = words_of[("wb", m)]
            columns = wb_grouped[:].bitcast(F32).rearrange(
                "p (c h q t) w -> p c h q (t w)", c=2, h=HEADS, t=PACK
            )
            words = bank[:].rearrange("p t w (h c q) -> p c h q (t w)", h=HEADS, c=2)
            run = slice(m * UNIT_TILES * 2, (m + 1) * UNIT_TILES * 2)
            copy = nc.vector.tensor_copy if m == 0 else nc.scalar.copy
            for c in range(2):
                copy(out=columns[:, c, :, :, run], in_=words[:, c])

        def quantise_weight(grouped, codes, scales, columns):
            nc.vector.quantize_mx(
                out=codes[:, columns].bitcast(FP8X4),
                scales=scales[:, columns],
                in_=grouped[:, columns, :].rearrange("p r t -> p (r t)"),
            )

        wa_scaled = keep.tile([P, PACK, K], BF16)
        wb_scaled = keep.tile([P, PACK, K], BF16)
        gain = keep.tile([P, K], BF16)
        wa_grouped = keep.tile([P, OUT, PACK], BF16, align_bytes=64)
        wa_codes = keep.tile([P, OUT], U32, align_bytes=64)
        wa_scales = keep.tile([P, OUT], U8, align_bytes=64)
        wb_grouped = keep.tile([P, OUT, PACK], BF16, align_bytes=64)
        wb_codes = keep.tile([P, OUT], U32, align_bytes=64)
        wb_scales = keep.tile([P, OUT], U8, align_bytes=64)

        def active(n):
            return 0 <= n < UNITS

        words_of = {}
        grouped_of = {}
        codes_of = {}
        lq_of = {}
        sums_of = {}
        inverse_of = {}
        rot_of = {}
        h_of = {}
        rope_of = {}
        plain_of = {}

        def transpose_unit(kind, n, rows):
            words_of[(kind, n)] = transpose_rows(kind, rows, kind == 1)

        def group_unit(kind, n):
            bank = words_of[(kind, n)]
            i = n + kind * Q_LAG
            if i not in grouped_of:
                grouped_of[i] = work.tile([P, 2, UNIT_TILES, P, PACK], BF16, name="grouped", align_bytes=64)
            nc.scalar.copy(
                out=grouped_of[i][:, kind].bitcast(F32), in_=bank[:].rearrange("p j u r -> p j r u")
            )

        def quantise(i):
            kinds = slice(0 if active(i) else 1, 2 if active(i - Q_LAG) else 1)
            codes = work.tile([P, 2, UNIT_TILES * P], U32, tag="codes", align_bytes=64)
            scales = work.tile([P, 2, UNIT_TILES * P], U8, tag="scales", align_bytes=64)
            nc.vector.quantize_mx(
                out=codes[:, kinds].rearrange("p k r -> p (k r)").bitcast(FP8X4),
                scales=scales[:, kinds].rearrange("p k r -> p (k r)"),
                in_=grouped_of[i][:, kinds].rearrange("p k j r t -> p (k j r t)"),
            )
            codes_of[i] = (codes, scales)

        def multiply(out, kind, n, j, w_codes, w_scales, columns):
            codes, scales = codes_of[n + kind * Q_LAG]
            tokens = slice(j * P, (j + 1) * P)
            nc.tensor.matmul_mx(
                out=out,
                lhsT=codes[:, kind, tokens].bitcast(FP8X4),
                lhsT_scale=scales[:, kind, tokens],
                rhs=w_codes[:, columns].bitcast(FP8X4),
                rhs_scale=w_scales[:, columns],
                start=True,
                stop=True,
            )

        def first_matmul(n):
            banks = []
            for j in range(UNIT_TILES):
                lq = psum_lq.tile([P, OUT], F32)
                multiply(lq[:], 0, n, j, wa_codes, wa_scales, slice(0, OUT))
                banks.append(lq)
            lq_of[n] = banks

        def sum_squares(n):
            sums = work.tile([P, UNIT_TILES], F32, tag="sums")
            for j in range(UNIT_TILES):
                squares = work.tile([P, OUT], BF16, tag="squares")
                nc.scalar.activation(
                    out=squares[:], in_=lq_of[n][j][:], func=ACT.Square, accum_out=sums[:, j : j + 1]
                )
            sums_of[n] = sums

        def invert(n):
            inverse = work.tile([P, UNIT_TILES], F32, tag="inverse")
            nc.scalar.activation(
                out=inverse[:], in_=sums_of[n][:], func=ACT.Abs_reciprocal_sqrt, bias=eps[:], scale=1.0 / OUT
            )
            inverse_of[n] = inverse

        def normalise(n):
            inverse = inverse_of[n]
            h = work.tile([P, UNIT_TILES, K], BF16, tag="h")
            banks = lq_of[n]
            for j in range(UNIT_TILES):
                nc.vector.scalar_tensor_tensor(
                    out=h[:, j, :],
                    in0=banks[j][:],
                    scalar=inverse[:, j : j + 1],
                    in1=gain[:],
                    op0=ALU.mult,
                    op1=ALU.mult,
                )
            h_of[n] = h

        def second_matmul_rotated(n):
            rope = psum_turns.tile([P, UNIT_TILES, HEADS, ROPE], F32, tag="turns")
            for j in range(UNIT_TILES):
                multiply(
                    rope[:, j].rearrange("p h d -> p (h d)"),
                    1, n, j, wb_codes, wb_scales, slice(HEADS * NOPE, OUT),
                )
            rope_of[n] = rope

        def second_matmul_plain(n):
            plain = psum_own.tile([P, UNIT_TILES, HEADS * NOPE], F32, tag="plain")
            for j in range(UNIT_TILES):
                multiply(plain[:, j, :], 1, n, j, wb_codes, wb_scales, slice(0, HEADS * NOPE))
            plain_of[n] = plain

        def store_plain(n):
            tiles = slice(n * UNIT_TILES, (n + 1) * UNIT_TILES)
            nope_sb = results.tile([P, UNIT_TILES, HEADS * NOPE], F32, tag="nope", bufs=UNITS)
            nc.scalar.copy(out=nope_sb[:], in_=plain_of[n][:])
            queue = nc.scalar if n == UNITS - 1 else nc.sync
            queue.dma_start(out=nope_dram[:, tiles, :], in_=nope_sb[:])

        def rotate(n, here, there, sum_op):
            first = (n * UNIT_TILES) % TABLE_TILES
            piece = (n * UNIT_TILES) // TABLE_TILES
            shape = [P, UNIT_TILES, HEADS, ROPE]
            cos_bc = cos_loads[piece][:, first : first + UNIT_TILES, :].unsqueeze(2).to_broadcast(shape)
            sin_bc = sin_loads[piece][:, first : first + UNIT_TILES, :].unsqueeze(2).to_broadcast(shape)
            rope = rope_of[n]
            half_shape = [P, UNIT_TILES, HEADS, HALF]
            straight = work.tile(half_shape, F32, tag="straight", bufs=PRODUCT_BUFS + 2)
            nc.vector.tensor_tensor(
                out=straight[:], in0=rope[:, :, :, here], in1=cos_bc[:, :, :, here], op=ALU.mult
            )
            crossed = work.tile(half_shape, F32, tag="crossed", bufs=PRODUCT_BUFS)
            nc.vector.tensor_tensor(
                out=crossed[:], in0=rope[:, :, :, there], in1=sin_bc[:, :, :, here], op=ALU.mult
            )

            def add_up(engine):
                engine.tensor_tensor(out=rot_of[n][:, :, :, here], in0=straight[:], in1=crossed[:], op=sum_op)

            return add_up

        def rotate_unit(n):
            rot_of[n] = results.tile([P, UNIT_TILES, HEADS, ROPE], F32, name="rot_sb", tag="rot", bufs=ROT_BUFS)
            add_low = rotate(n, LOW, HIGH, ALU.subtract)
            if n < UNITS - 1:
                add_low(nc.gpsimd)
            add_high = rotate(n, HIGH, LOW, ALU.add)
            if n < UNITS - 1:
                add_high(nc.gpsimd)
            else:
                add_low(nc.vector)
                add_high(nc.vector)
            tiles = slice(n * UNIT_TILES, (n + 1) * UNIT_TILES)
            nc.sync.dma_start(out=rot_dram[:, tiles, :], in_=rot_of[n][:].rearrange("p t h d -> p t (h d)"))

        wa_factors = own_factors(nc.vector, "wa", wa_all_factors)
        for m in range(WEIGHT_HALVES):
            scale_weight(wa_scaled, wa_raw, wa_factors, slice(m * UNIT_TILES, (m + 1) * UNIT_TILES))
        for m in range(WEIGHT_HALVES):
            transpose_wa(m)
        for m in range(WEIGHT_HALVES):
            quantise_weight(wa_grouped, wa_codes, wa_scales, slice(m * HALF_OUT, (m + 1) * HALF_OUT))
        for n in range(X_LEAD):
            transpose_unit(0, n, x_loads[n][:])
            group_unit(0, n)
        gain_bank = psum_own.tile([P, K], F32, tag="plain")
        nc.tensor.matmul(gain_bank[:], lhsT=ones[:, :P], rhs=gain_row[:], start=True, stop=True)

        nc.scalar.copy(
            out=gain[:].rearrange("p (u q e) -> p u q e", u=HALVES, e=2),
            in_=gain_bank[:].rearrange("p (q u e) -> p u q e", u=HALVES, e=2),
        )

        for i in range(UNITS + ROTATE_LAG):
            if active(i + LOAD_LEAD):
                load_ahead(i + LOAD_LEAD)
            if active(i) or active(i - Q_LAG):
                quantise(i)
            if i == Q_LAG:
                quantise_weight(wb_grouped, wb_codes, wb_scales, slice(0, OUT))
            if i == 0:
                scale_weight(wb_scaled, wb_raw, own_factors(nc.gpsimd, "wb", wb_all_factors), slice(0, PACK))
            if active(i - ROTATE_LAG):
                rotate_unit(i - ROTATE_LAG)
            if i == 1:
                group_wb(0)
            if active(i - 1):
                normalise(i - 1)
            if active(i):
                first_matmul(i)
            if active(i - Q_LAG):
                second_matmul_plain(i - Q_LAG)
                second_matmul_rotated(i - Q_LAG)
            if active(i + X_LEAD):
                transpose_unit(0, i + X_LEAD, x_loads[i + X_LEAD][:])
            if active(i - 1):
                transpose_unit(1, i - 1, h_of[i - 1][:])
            if i < WEIGHT_HALVES:
                transpose_wb(i)
            if i == 2:
                group_wb(1)
            if active(i):
                sum_squares(i)
            if active(i - Q_LAG):
                store_plain(i - Q_LAG)
            if active(i):
                invert(i)
            if active(i + X_LEAD):
                group_unit(0, i + X_LEAD)
            if active(i - 1):
                group_unit(1, i - 1)
